import numpy as np
import ml_dtypes


def mxq(x, axis, fmt="e4m3"):
    dtype, down = {"e4m3": (ml_dtypes.float8_e4m3fn, 7), "e5m2": (ml_dtypes.float8_e5m2, 14)}[fmt]
    v = np.moveaxis(np.asarray(x, np.float32).astype(ml_dtypes.bfloat16).astype(np.float64), axis, -1)
    blocks = v.reshape(v.shape[:-1] + (-1, 32))
    amax = np.abs(blocks).max(-1, keepdims=True)
    byte = np.maximum(np.where(amax > 0, np.frexp(amax)[1] - 1 + 127, 0) - down, 1)
    scale = np.exp2(byte - 127.0)
    codes = (blocks / scale).astype(np.float32).astype(dtype).astype(np.float64)
    return np.moveaxis((codes * scale).reshape(v.shape), -1, axis)


WIDE = False


def mx_kscale(k):
    if not WIDE:
        return np.ones(k)
    levels = np.array([10, -10, 5, -5, 0])
    a = np.random.permutation(np.resize(levels, k // 512 * 4)).reshape(k // 512, 4)
    idx = np.arange(k)
    return np.exp2(a[idx // 512, idx % 128 // 32])


BF16 = ml_dtypes.bfloat16


def bf(x):
    return np.asarray(x, np.float32).astype(BF16)


def f64(x):
    return np.asarray(x).astype(np.float64)


B, N, D = 4, 1024, 512
BN = B * N
DM = D + D


def sigmoid(v):
    return 1.0 / (1.0 + np.exp(-v))


def setup_inputs():
    s = mx_kscale(DM)
    return {"node_state": bf(np.random.standard_normal((B, N, D))),
            "message": bf(np.random.standard_normal((B, N, DM)) * s),
            "h_tilda": bf(np.tanh(np.random.standard_normal((BN, D)))),
            "mask": bf(np.random.uniform(size=(B, N)) < 0.9),
            "w_z": bf(np.random.standard_normal((DM, D)) / np.sqrt(DM) / s[:, None]),
            "u_z": bf(np.random.standard_normal((D, D)) / np.sqrt(D))}


def reference(node_state, message, h_tilda, mask, w_z, u_z):
    h = f64(node_state).reshape(BN, D)
    m = f64(message).reshape(BN, DM)
    z_t = sigmoid((mxq(m, 1, "e4m3") @ mxq(f64(w_z), 0, "e4m3")) + (mxq(h, 1, "e4m3") @ mxq(f64(u_z), 0, "e4m3")))
    h_t = (1.0 - z_t) * h + z_t * f64(h_tilda)
    h_t = h_t * f64(mask).reshape(BN)[:, None]
    return h_t.reshape(B, N, D)

@@ -1,0 +1,206 @@
+import concourse.mybir as mybir
+from concourse.masks import make_identity
+
+F32 = mybir.dt.float32
+BF16 = mybir.dt.bfloat16
+U32 = mybir.dt.uint32
+U8 = mybir.dt.uint8
+FP8X4 = mybir.dt.float8_e4m3fn_x4
+ALU = mybir.AluOpType
+ACT = mybir.ActivationFunctionType
+
+P = 128
+PACK = 4
+K_PASS = P * PACK
+HALVES = 2
+
+ROWS = 4096
+D = 512
+DM = 1024
+M_PASSES = DM // K_PASS
+PASSES = M_PASSES + D // K_PASS
+
+TILES = ROWS // P
+PAIR = 2
+PAIRS = TILES // PAIR
+SLOTS = PAIR * PASSES
+SLOTS_PER_BANK = 2
+BANKS = SLOTS // SLOTS_PER_BANK
+BANK_K = SLOTS_PER_BANK * P * PACK
+
+CHUNK_TILES = 4
+CHUNK_PAIRS = CHUNK_TILES // PAIR
+CHUNKS = TILES // CHUNK_TILES
+LOAD_AHEAD = 3
+
+FLOPS = 2 * ROWS * (DM + D) * D
+
+
+def tile_updatefunction_pb_t_kernel(tc, node_state, message, h_tilda, mask, w_z, u_z, out):
+    nc = tc.nc
+
+    m_rows = message.rearrange("b (q t) k -> (b q) t k", t=TILES)
+    h_rows = node_state.rearrange("b (q t) d -> (b q) t d", t=TILES)
+    ht_rows = h_tilda.rearrange("(p t) d -> p t d", t=TILES)
+    mask_rows = mask.rearrange("b (q t) -> (b q) t", t=TILES)
+    out_rows = out.rearrange("b (q t) d -> (b q) t d", t=TILES)
+
+    with (
+        tc.manual_schedule(),
+        tc.tile_pool(name="consts", bufs=1) as consts,
+        tc.tile_pool(name="inputs", bufs=1) as inputs,
+        tc.tile_pool(name="grouped", bufs=3) as grouped_pool,
+        tc.tile_pool(name="packed", bufs=3) as packed_pool,
+        tc.tile_pool(name="gates", bufs=3) as gate_pool,
+        tc.tile_pool(name="blends", bufs=6) as blend_pool,
+        tc.psum_pool(name="transposed", bufs=4) as transposed_pool,
+        tc.psum_pool(name="sums", bufs=4) as sum_pool,
+    ):
+        m_chunks, h_chunks, ht_chunks = {}, {}, {}
+        grouped_of, codes_of, scales_of, gate_of, blend_of = {}, {}, {}, {}, {}
+
+        def load_chunk(c):
+            tiles = slice(c * CHUNK_TILES, (c + 1) * CHUNK_TILES)
+            m_chunks[c] = inputs.tile([P, CHUNK_TILES, DM], BF16, name="m%d" % c)
+            h_chunks[c] = inputs.tile([P, CHUNK_TILES, D], BF16, name="h%d" % c)
+            ht_chunks[c] = inputs.tile([P, CHUNK_TILES, D], BF16, name="ht%d" % c)
+            nc.sync.dma_start(out=m_chunks[c][:], in_=m_rows[:, tiles, :])
+            nc.sync.dma_start(out=h_chunks[c][:], in_=h_rows[:, tiles, :])
+            nc.sync.dma_start(out=ht_chunks[c][:], in_=ht_rows[:, tiles, :])
+
+        def k_slab(t, g):
+            c, local = divmod(t, CHUNK_TILES)
+            if g < M_PASSES:
+                return m_chunks[c][:, local, g * K_PASS : (g + 1) * K_PASS]
+            return h_chunks[c][:, local, :]
+
+        def transpose_pair(i):
+            grouped = grouped_pool.tile([P, BANKS * BANK_K], BF16, name="grouped", align_bytes=64)
+            grouped_of[i] = grouped
+            for bank in range(BANKS):
+                xt = transposed_pool.tile([P, SLOTS_PER_BANK, HALVES, P], F32, name="xt")
+                for o in range(SLOTS_PER_BANK):
+                    local, g = divmod(bank * SLOTS_PER_BANK + o, PASSES)
+                    words = k_slab(PAIR * i + local, g).bitcast(F32)
+                    for u in range(HALVES):
+                        nc.tensor.transpose(xt[:, o, u, :], words[:, u * P : (u + 1) * P], identity[:])
+                nc.scalar.copy(
+                    out=grouped[:, bank * BANK_K : (bank + 1) * BANK_K]
+                    .bitcast(F32)
+                    .rearrange("p (o r u) -> p o r u", o=SLOTS_PER_BANK, u=HALVES),
+                    in_=xt[:].rearrange("p o u r -> p o r u"),
+                )
+
+        def quantise_pair(i):
+            codes = packed_pool.tile([P, SLOTS * P], U32, name="codes", align_bytes=64)
+            scales = packed_pool.tile([P, SLOTS * P], U8, name="scales", align_bytes=64)
+            codes_of[i], scales_of[i] = codes, scales
+            for bank in range(BANKS):
+                columns = slice(bank * SLOTS_PER_BANK * P, (bank + 1) * SLOTS_PER_BANK * P)
+                nc.vector.quantize_mx(
+                    out=codes[:, columns].bitcast(FP8X4),
+                    scales=scales[:, columns],
+                    in_=grouped_of[i][:, bank * BANK_K : (bank + 1) * BANK_K],
+                )
+
+        def multiply_pair(i):
+            gate = gate_pool.tile([P, PAIR, D], F32, name="gate")
+            gate_of[i] = gate
+            for local in range(PAIR):
+                acc = sum_pool.tile([P, D], F32, name="acc")
+                for g in range(PASSES):
+                    rows = slice((local * PASSES + g) * P, (local * PASSES + g + 1) * P)
+                    nc.tensor.matmul_mx(
+                        out=acc[:],
+                        lhsT=codes_of[i][:, rows].bitcast(FP8X4),
+                        lhsT_scale=scales_of[i][:, rows],
+                        rhs=w_codes[:, g, :].bitcast(FP8X4),
+                        rhs_scale=w_scales[:, g, :],
+                        start=(g == 0),
+                        stop=(g == PASSES - 1),
+                    )
+                nc.scalar.activation(out=gate[:, local, :], in_=acc[:], func=ACT.Sigmoid)
+
+        def pair_of(chunks, i):
+            c, first = divmod(PAIR * i, CHUNK_TILES)
+            return chunks[c][:, first : first + PAIR, :]
+
+        def difference_pair(i):
+            blend = blend_pool.tile([P, PAIR, D], F32, name="blend")
+            blend_of[i] = blend
+            nc.vector.tensor_tensor(
+                out=blend[:], in0=pair_of(ht_chunks, i), in1=pair_of(h_chunks, i), op=ALU.subtract
+            )
+
+        def blend_pair(i):
+            blend, gate, h_pair = blend_of[i], gate_of[i], pair_of(h_chunks, i)
+            for local in range(PAIR):
+                t = PAIR * i + local
+                nc.vector.scalar_tensor_tensor(
+                    out=blend[:, local, :],
+                    in0=gate[:, local, :],
+                    scalar=mask_f32[:, t : t + 1],
+                    in1=blend[:, local, :],
+                    op0=ALU.mult,
+                    op1=ALU.mult,
+                )
+            for local in range(PAIR):
+                t = PAIR * i + local
+                nc.vector.scalar_tensor_tensor(
+                    out=blend[:, local, :],
+                    in0=h_pair[:, local, :],
+                    scalar=mask_f32[:, t : t + 1],
+                    in1=blend[:, local, :],
+                    op0=ALU.mult,
+                    op1=ALU.add,
+                )
+            nc.sync.dma_start(out=out_rows[:, PAIR * i : PAIR * (i + 1), :], in_=blend[:])
+
+        w_raw = consts.tile([P, PASSES, PACK, D], BF16)
+        nc.sync.dma_start(
+            out=w_raw[:, 0:M_PASSES].rearrange("p g (u e) c -> p (g u) (e c)", e=2),
+            in_=w_z.rearrange("(a p e) c -> p a (e c)", p=P, e=2),
+        )
+        nc.sync.dma_start(
+            out=w_raw[:, M_PASSES].rearrange("p (u e) c -> p u (e c)", e=2),
+            in_=u_z.rearrange("(u p e) c -> p u (e c)", p=P, e=2),
+        )
+        mask_bf16 = consts.tile([P, TILES], BF16)
+        nc.sync.dma_start(out=mask_bf16[:], in_=mask_rows)
+        for c in range(LOAD_AHEAD):
+            load_chunk(c)
+
+        identity = consts.tile([P, P], F32)
+        make_identity(nc, identity[:])
+        warm = consts.tile([P, 1], F32)
+        nc.vector.memset(warm[:], 0.0)
+        nc.scalar.activation(out=warm[:], in_=warm[:], func=ACT.Sigmoid)
+
+        w_grouped = consts.tile([P, PASSES, D, PACK], BF16, align_bytes=64)
+        w_codes = consts.tile([P, PASSES, D], U32, align_bytes=64)
+        w_scales = consts.tile([P, PASSES, D], U8, align_bytes=64)
+        for g in range(M_PASSES):
+            nc.vector.tensor_copy(out=w_grouped[:, g], in_=w_raw[:, g].rearrange("p t c -> p c t"))
+        nc.scalar.copy(out=w_grouped[:, M_PASSES], in_=w_raw[:, M_PASSES].rearrange("p t c -> p c t"))
+        mask_f32 = consts.tile([P, TILES], F32)
+        nc.vector.tensor_copy(out=mask_f32[:], in_=mask_bf16[:])
+        for g in range(PASSES):
+            nc.vector.quantize_mx(
+                out=w_codes[:, g, :].bitcast(FP8X4),
+                scales=w_scales[:, g, :],
+                in_=w_grouped[:, g].rearrange("p c t -> p (c t)"),
+            )
+
+        for i in range(PAIRS + 2):
+            c_next = i // CHUNK_PAIRS + LOAD_AHEAD
+            if i % CHUNK_PAIRS == 0 and c_next < CHUNKS:
+                load_chunk(c_next)
+            if i < PAIRS:
+                transpose_pair(i)
+            if 1 <= i <= PAIRS:
+                multiply_pair(i - 1)
+            if i >= 2:
+                blend_pair(i - 2)
+            if i < PAIRS:
+                difference_pair(i)
+                quantise_pair(i)

@@ -53,20 +53,23 @@ def tile_updatefunction_pb_t_kernel(tc, node_state, message, h_tilda, mask, w_z,
         tc.tile_pool(name="packed", bufs=3) as packed_pool,
         tc.tile_pool(name="gates", bufs=3) as gate_pool,
         tc.tile_pool(name="blends", bufs=6) as blend_pool,
-        tc.psum_pool(name="transposed", bufs=4) as transposed_pool,
-        tc.psum_pool(name="sums", bufs=4) as sum_pool,
+        tc.psum_pool(name="transposed", bufs=BANKS) as transposed_pool,
+        tc.psum_pool(name="sums", bufs=3) as sum_pool,
+        tc.psum_pool(name="differences", bufs=2) as difference_pool,
     ):
         m_chunks, h_chunks, ht_chunks = {}, {}, {}
-        grouped_of, codes_of, scales_of, gate_of, blend_of = {}, {}, {}, {}, {}
+        grouped_of, codes_of, scales_of, gate_of, blend_of, first_difference_of = {}, {}, {}, {}, {}, {}
 
-        def load_chunk(c):
-            tiles = slice(c * CHUNK_TILES, (c + 1) * CHUNK_TILES)
+        def load_chunk(c, piece_tiles):
             m_chunks[c] = inputs.tile([P, CHUNK_TILES, DM], BF16, name="m%d" % c)
             h_chunks[c] = inputs.tile([P, CHUNK_TILES, D], BF16, name="h%d" % c)
             ht_chunks[c] = inputs.tile([P, CHUNK_TILES, D], BF16, name="ht%d" % c)
-            nc.sync.dma_start(out=m_chunks[c][:], in_=m_rows[:, tiles, :])
-            nc.sync.dma_start(out=h_chunks[c][:], in_=h_rows[:, tiles, :])
-            nc.sync.dma_start(out=ht_chunks[c][:], in_=ht_rows[:, tiles, :])
+            for first in range(0, CHUNK_TILES, piece_tiles):
+                local = slice(first, first + piece_tiles)
+                tiles = slice(c * CHUNK_TILES + first, c * CHUNK_TILES + first + piece_tiles)
+                nc.sync.dma_start(out=m_chunks[c][:, local, :], in_=m_rows[:, tiles, :])
+                nc.sync.dma_start(out=h_chunks[c][:, local, :], in_=h_rows[:, tiles, :])
+                nc.sync.dma_start(out=ht_chunks[c][:, local, :], in_=ht_rows[:, tiles, :])
 
         def k_slab(t, g):
             c, local = divmod(t, CHUNK_TILES)
@@ -125,22 +128,33 @@ def tile_updatefunction_pb_t_kernel(tc, node_state, message, h_tilda, mask, w_z,
             c, first = divmod(PAIR * i, CHUNK_TILES)
             return chunks[c][:, first : first + PAIR, :]
 
-        def difference_pair(i):
+        def difference_on_tensor(i):
+            difference = difference_pool.tile([P, D], F32, name="difference")
+            first_difference_of[i] = difference
+            nc.tensor.matmul(
+                out=difference[:], lhsT=plus_identity[:], rhs=pair_of(ht_chunks, i)[:, 0, :], start=True, stop=False
+            )
+            nc.tensor.matmul(
+                out=difference[:], lhsT=minus_identity[:], rhs=pair_of(h_chunks, i)[:, 0, :], start=False, stop=True
+            )
+
+        def difference_on_vector(i):
             blend = blend_pool.tile([P, PAIR, D], F32, name="blend")
             blend_of[i] = blend
             nc.vector.tensor_tensor(
-                out=blend[:], in0=pair_of(ht_chunks, i), in1=pair_of(h_chunks, i), op=ALU.subtract
+                out=blend[:, 1, :], in0=pair_of(ht_chunks, i)[:, 1, :], in1=pair_of(h_chunks, i)[:, 1, :], op=ALU.subtract
             )
 
         def blend_pair(i):
             blend, gate, h_pair = blend_of[i], gate_of[i], pair_of(h_chunks, i)
+            differences = [first_difference_of[i][:], blend[:, 1, :]]
             for local in range(PAIR):
                 t = PAIR * i + local
                 nc.vector.scalar_tensor_tensor(
                     out=blend[:, local, :],
                     in0=gate[:, local, :],
                     scalar=mask_f32[:, t : t + 1],
-                    in1=blend[:, local, :],
+                    in1=differences[local],
                     op0=ALU.mult,
                     op1=ALU.mult,
                 )
@@ -157,21 +171,24 @@ def tile_updatefunction_pb_t_kernel(tc, node_state, message, h_tilda, mask, w_z,
             nc.sync.dma_start(out=out_rows[:, PAIR * i : PAIR * (i + 1), :], in_=blend[:])
 
         w_raw = consts.tile([P, PASSES, PACK, D], BF16)
-        nc.sync.dma_start(
-            out=w_raw[:, 0:M_PASSES].rearrange("p g (u e) c -> p (g u) (e c)", e=2),
-            in_=w_z.rearrange("(a p e) c -> p a (e c)", p=P, e=2),
-        )
-        nc.sync.dma_start(
-            out=w_raw[:, M_PASSES].rearrange("p (u e) c -> p u (e c)", e=2),
-            in_=u_z.rearrange("(u p e) c -> p u (e c)", p=P, e=2),
-        )
+        pass_rows = [w_z[g * K_PASS : (g + 1) * K_PASS, :] for g in range(M_PASSES)] + [u_z]
+        for g in range(PASSES):
+            nc.sync.dma_start(
+                out=w_raw[:, g].rearrange("p (u e) c -> p u (e c)", e=2),
+                in_=pass_rows[g].rearrange("(u p e) c -> p u (e c)", p=P, e=2),
+            )
         mask_bf16 = consts.tile([P, TILES], BF16)
         nc.sync.dma_start(out=mask_bf16[:], in_=mask_rows)
-        for c in range(LOAD_AHEAD):
-            load_chunk(c)
+        load_chunk(0, piece_tiles=PAIR)
+        for c in range(1, LOAD_AHEAD):
+            load_chunk(c, piece_tiles=CHUNK_TILES)
 
         identity = consts.tile([P, P], F32)
         make_identity(nc, identity[:])
+        plus_identity = consts.tile([P, P], BF16)
+        make_identity(nc, plus_identity[:])
+        minus_identity = consts.tile([P, P], BF16)
+        nc.vector.tensor_scalar_mul(out=minus_identity[:], in0=plus_identity[:], scalar1=-1.0)
         warm = consts.tile([P, 1], F32)
         nc.vector.memset(warm[:], 0.0)
         nc.scalar.activation(out=warm[:], in_=warm[:], func=ACT.Sigmoid)
@@ -194,13 +211,14 @@ def tile_updatefunction_pb_t_kernel(tc, node_state, message, h_tilda, mask, w_z,
         for i in range(PAIRS + 2):
             c_next = i // CHUNK_PAIRS + LOAD_AHEAD
             if i % CHUNK_PAIRS == 0 and c_next < CHUNKS:
-                load_chunk(c_next)
+                load_chunk(c_next, piece_tiles=CHUNK_TILES)
             if i < PAIRS:
                 transpose_pair(i)
             if 1 <= i <= PAIRS:
+                difference_on_tensor(i - 1)
                 multiply_pair(i - 1)
             if i >= 2:
                 blend_pair(i - 2)
             if i < PAIRS:
-                difference_pair(i)
+                difference_on_vector(i)
                 quantise_pair(i)

@@ -32,6 +32,7 @@ CHUNK_TILES = 4
 CHUNK_PAIRS = CHUNK_TILES // PAIR
 CHUNKS = TILES // CHUNK_TILES
 LOAD_AHEAD = 3
+W_VECTOR_COLUMNS = 336
 
 FLOPS = 2 * ROWS * (DM + D) * D
 
@@ -98,12 +99,12 @@ def tile_updatefunction_pb_t_kernel(tc, node_state, message, h_tilda, mask, w_z,
             codes = packed_pool.tile([P, SLOTS * P], U32, name="codes", align_bytes=64)
             scales = packed_pool.tile([P, SLOTS * P], U8, name="scales", align_bytes=64)
             codes_of[i], scales_of[i] = codes, scales
-            for bank in range(BANKS):
-                columns = slice(bank * SLOTS_PER_BANK * P, (bank + 1) * SLOTS_PER_BANK * P)
+            for first_bank, end_bank in ((0, 2), (2, BANKS)):
+                columns = slice(first_bank * SLOTS_PER_BANK * P, end_bank * SLOTS_PER_BANK * P)
                 nc.vector.quantize_mx(
                     out=codes[:, columns].bitcast(FP8X4),
                     scales=scales[:, columns],
-                    in_=grouped_of[i][:, bank * BANK_K : (bank + 1) * BANK_K],
+                    in_=grouped_of[i][:, first_bank * BANK_K : end_bank * BANK_K],
                 )
 
         def multiply_pair(i):
@@ -168,8 +169,10 @@ def tile_updatefunction_pb_t_kernel(tc, node_state, message, h_tilda, mask, w_z,
                     op0=ALU.mult,
                     op1=ALU.add,
                 )
-            nc.sync.dma_start(out=out_rows[:, PAIR * i : PAIR * (i + 1), :], in_=blend[:])
+                nc.sync.dma_start(out=out_rows[:, t, :], in_=blend[:, local, :])
 
+        mask_bf16 = consts.tile([P, TILES], BF16)
+        nc.sync.dma_start(out=mask_bf16[:], in_=mask_rows)
         w_raw = consts.tile([P, PASSES, PACK, D], BF16)
         pass_rows = [w_z[g * K_PASS : (g + 1) * K_PASS, :] for g in range(M_PASSES)] + [u_z]
         for g in range(PASSES):
@@ -177,8 +180,6 @@ def tile_updatefunction_pb_t_kernel(tc, node_state, message, h_tilda, mask, w_z,
                 out=w_raw[:, g].rearrange("p (u e) c -> p u (e c)", e=2),
                 in_=pass_rows[g].rearrange("(u p e) c -> p u (e c)", p=P, e=2),
             )
-        mask_bf16 = consts.tile([P, TILES], BF16)
-        nc.sync.dma_start(out=mask_bf16[:], in_=mask_rows)
         load_chunk(0, piece_tiles=PAIR)
         for c in range(1, LOAD_AHEAD):
             load_chunk(c, piece_tiles=CHUNK_TILES)
@@ -193,20 +194,29 @@ def tile_updatefunction_pb_t_kernel(tc, node_state, message, h_tilda, mask, w_z,
         nc.vector.memset(warm[:], 0.0)
         nc.scalar.activation(out=warm[:], in_=warm[:], func=ACT.Sigmoid)
 
+        mask_f32 = consts.tile([P, TILES], F32)
+        nc.vector.tensor_copy(out=mask_f32[:], in_=mask_bf16[:])
         w_grouped = consts.tile([P, PASSES, D, PACK], BF16, align_bytes=64)
         w_codes = consts.tile([P, PASSES, D], U32, align_bytes=64)
         w_scales = consts.tile([P, PASSES, D], U8, align_bytes=64)
-        for g in range(M_PASSES):
-            nc.vector.tensor_copy(out=w_grouped[:, g], in_=w_raw[:, g].rearrange("p t c -> p c t"))
-        nc.scalar.copy(out=w_grouped[:, M_PASSES], in_=w_raw[:, M_PASSES].rearrange("p t c -> p c t"))
-        mask_f32 = consts.tile([P, TILES], F32)
-        nc.vector.tensor_copy(out=mask_f32[:], in_=mask_bf16[:])
-        for g in range(PASSES):
+
+        def regroup_weights(g):
+            by_column = w_raw[:, g].rearrange("p t c -> p c t")
+            nc.vector.tensor_copy(out=w_grouped[:, g, :W_VECTOR_COLUMNS], in_=by_column[:, :W_VECTOR_COLUMNS])
+            nc.scalar.copy(out=w_grouped[:, g, W_VECTOR_COLUMNS:], in_=by_column[:, W_VECTOR_COLUMNS:])
+
+        def quantise_weights(g):
             nc.vector.quantize_mx(
                 out=w_codes[:, g, :].bitcast(FP8X4),
                 scales=w_scales[:, g, :],
                 in_=w_grouped[:, g].rearrange("p c t -> p (c t)"),
             )
+
+        regroup_weights(0)
+        for g in range(1, PASSES):
+            regroup_weights(g)
+            quantise_weights(g - 1)
+        quantise_weights(PASSES - 1)
 
         for i in range(PAIRS + 2):
             c_next = i // CHUNK_PAIRS + LOAD_AHEAD

@@ -129,14 +129,20 @@ def tile_updatefunction_pb_t_kernel(tc, node_state, message, h_tilda, mask, w_z,
             c, first = divmod(PAIR * i, CHUNK_TILES)
             return chunks[c][:, first : first + PAIR, :]
 
-        def difference_on_tensor(i):
+        def open_difference_on_tensor(i):
             difference = difference_pool.tile([P, D], F32, name="difference")
             first_difference_of[i] = difference
             nc.tensor.matmul(
                 out=difference[:], lhsT=plus_identity[:], rhs=pair_of(ht_chunks, i)[:, 0, :], start=True, stop=False
             )
+
+        def close_difference_on_tensor(i):
             nc.tensor.matmul(
-                out=difference[:], lhsT=minus_identity[:], rhs=pair_of(h_chunks, i)[:, 0, :], start=False, stop=True
+                out=first_difference_of[i][:],
+                lhsT=minus_identity[:],
+                rhs=pair_of(h_chunks, i)[:, 0, :],
+                start=False,
+                stop=True,
             )
 
         def difference_on_vector(i):
@@ -225,8 +231,9 @@ def tile_updatefunction_pb_t_kernel(tc, node_state, message, h_tilda, mask, w_z,
             if i < PAIRS:
                 transpose_pair(i)
             if 1 <= i <= PAIRS:
-                difference_on_tensor(i - 1)
+                open_difference_on_tensor(i - 1)
                 multiply_pair(i - 1)
+                close_difference_on_tensor(i - 1)
             if i >= 2:
                 blend_pair(i - 2)
             if i < PAIRS:

@@ -59,7 +59,7 @@ def tile_updatefunction_pb_t_kernel(tc, node_state, message, h_tilda, mask, w_z,
         tc.psum_pool(name="differences", bufs=2) as difference_pool,
     ):
         m_chunks, h_chunks, ht_chunks = {}, {}, {}
-        grouped_of, codes_of, scales_of, gate_of, blend_of, first_difference_of = {}, {}, {}, {}, {}, {}
+        grouped_of, codes_of, scales_of, gate_of, blend_of, tensor_difference_of = {}, {}, {}, {}, {}, {}
 
         def load_chunk(c, piece_tiles):
             m_chunks[c] = inputs.tile([P, CHUNK_TILES, DM], BF16, name="m%d" % c)
@@ -125,36 +125,52 @@ def tile_updatefunction_pb_t_kernel(tc, node_state, message, h_tilda, mask, w_z,
                     )
                 nc.scalar.activation(out=gate[:, local, :], in_=acc[:], func=ACT.Sigmoid)
 
+        def tensor_tiles(i):
+            return PAIR if i % 5 == 0 and i > 0 else 1
+
         def pair_of(chunks, i):
             c, first = divmod(PAIR * i, CHUNK_TILES)
             return chunks[c][:, first : first + PAIR, :]
 
         def open_difference_on_tensor(i):
-            difference = difference_pool.tile([P, D], F32, name="difference")
-            first_difference_of[i] = difference
-            nc.tensor.matmul(
-                out=difference[:], lhsT=plus_identity[:], rhs=pair_of(ht_chunks, i)[:, 0, :], start=True, stop=False
-            )
+            for local in range(tensor_tiles(i)):
+                difference = difference_pool.tile([P, D], F32, name="difference")
+                tensor_difference_of[i, local] = difference
+                nc.tensor.matmul(
+                    out=difference[:],
+                    lhsT=plus_identity[:],
+                    rhs=pair_of(ht_chunks, i)[:, local, :],
+                    start=True,
+                    stop=False,
+                )
 
         def close_difference_on_tensor(i):
-            nc.tensor.matmul(
-                out=first_difference_of[i][:],
-                lhsT=minus_identity[:],
-                rhs=pair_of(h_chunks, i)[:, 0, :],
-                start=False,
-                stop=True,
-            )
+            for local in range(tensor_tiles(i)):
+                nc.tensor.matmul(
+                    out=tensor_difference_of[i, local][:],
+                    lhsT=minus_identity[:],
+                    rhs=pair_of(h_chunks, i)[:, local, :],
+                    start=False,
+                    stop=True,
+                )
 
         def difference_on_vector(i):
             blend = blend_pool.tile([P, PAIR, D], F32, name="blend")
             blend_of[i] = blend
-            nc.vector.tensor_tensor(
-                out=blend[:, 1, :], in0=pair_of(ht_chunks, i)[:, 1, :], in1=pair_of(h_chunks, i)[:, 1, :], op=ALU.subtract
-            )
+            if tensor_tiles(i) < PAIR:
+                nc.vector.tensor_tensor(
+                    out=blend[:, 1, :],
+                    in0=pair_of(ht_chunks, i)[:, 1, :],
+                    in1=pair_of(h_chunks, i)[:, 1, :],
+                    op=ALU.subtract,
+                )
 
         def blend_pair(i):
             blend, gate, h_pair = blend_of[i], gate_of[i], pair_of(h_chunks, i)
-            differences = [first_difference_of[i][:], blend[:, 1, :]]
+            differences = [
+                tensor_difference_of[i, local][:] if local < tensor_tiles(i) else blend[:, local, :]
+                for local in range(PAIR)
+            ]
             for local in range(PAIR):
                 t = PAIR * i + local
                 nc.vector.scalar_tensor_tensor(

@@ -55,22 +55,27 @@ def tile_updatefunction_pb_t_kernel(tc, node_state, message, h_tilda, mask, w_z,
         tc.tile_pool(name="gates", bufs=3) as gate_pool,
         tc.tile_pool(name="blends", bufs=6) as blend_pool,
         tc.psum_pool(name="transposed", bufs=BANKS) as transposed_pool,
-        tc.psum_pool(name="sums", bufs=3) as sum_pool,
-        tc.psum_pool(name="differences", bufs=2) as difference_pool,
+        tc.psum_pool(name="sums", bufs=PAIR) as sum_pool,
+        tc.psum_pool(name="differences", bufs=3) as difference_pool,
     ):
         m_chunks, h_chunks, ht_chunks = {}, {}, {}
         grouped_of, codes_of, scales_of, gate_of, blend_of, tensor_difference_of = {}, {}, {}, {}, {}, {}
 
-        def load_chunk(c, piece_tiles):
+        def open_chunk(c):
             m_chunks[c] = inputs.tile([P, CHUNK_TILES, DM], BF16, name="m%d" % c)
             h_chunks[c] = inputs.tile([P, CHUNK_TILES, D], BF16, name="h%d" % c)
             ht_chunks[c] = inputs.tile([P, CHUNK_TILES, D], BF16, name="ht%d" % c)
-            for first in range(0, CHUNK_TILES, piece_tiles):
-                local = slice(first, first + piece_tiles)
-                tiles = slice(c * CHUNK_TILES + first, c * CHUNK_TILES + first + piece_tiles)
-                nc.sync.dma_start(out=m_chunks[c][:, local, :], in_=m_rows[:, tiles, :])
-                nc.sync.dma_start(out=h_chunks[c][:, local, :], in_=h_rows[:, tiles, :])
-                nc.sync.dma_start(out=ht_chunks[c][:, local, :], in_=ht_rows[:, tiles, :])
+
+        def load_rows(chunks, rows, first_tile, count):
+            c, first = divmod(first_tile, CHUNK_TILES)
+            nc.sync.dma_start(
+                out=chunks[c][:, first : first + count, :], in_=rows[:, first_tile : first_tile + count, :]
+            )
+
+        def load_chunk(c):
+            open_chunk(c)
+            for chunks, rows in ((m_chunks, m_rows), (h_chunks, h_rows), (ht_chunks, ht_rows)):
+                load_rows(chunks, rows, c * CHUNK_TILES, CHUNK_TILES)
 
         def k_slab(t, g):
             c, local = divmod(t, CHUNK_TILES)
@@ -78,34 +83,36 @@ def tile_updatefunction_pb_t_kernel(tc, node_state, message, h_tilda, mask, w_z,
                 return m_chunks[c][:, local, g * K_PASS : (g + 1) * K_PASS]
             return h_chunks[c][:, local, :]
 
-        def transpose_pair(i):
-            grouped = grouped_pool.tile([P, BANKS * BANK_K], BF16, name="grouped", align_bytes=64)
-            grouped_of[i] = grouped
-            for bank in range(BANKS):
-                xt = transposed_pool.tile([P, SLOTS_PER_BANK, HALVES, P], F32, name="xt")
-                for o in range(SLOTS_PER_BANK):
-                    local, g = divmod(bank * SLOTS_PER_BANK + o, PASSES)
-                    words = k_slab(PAIR * i + local, g).bitcast(F32)
-                    for u in range(HALVES):
-                        nc.tensor.transpose(xt[:, o, u, :], words[:, u * P : (u + 1) * P], identity[:])
-                nc.scalar.copy(
-                    out=grouped[:, bank * BANK_K : (bank + 1) * BANK_K]
-                    .bitcast(F32)
-                    .rearrange("p (o r u) -> p o r u", o=SLOTS_PER_BANK, u=HALVES),
-                    in_=xt[:].rearrange("p o u r -> p o r u"),
-                )
+        def slot_of(local, g):
+            return local * M_PASSES + g if g < M_PASSES else PAIR * M_PASSES + local
 
-        def quantise_pair(i):
-            codes = packed_pool.tile([P, SLOTS * P], U32, name="codes", align_bytes=64)
-            scales = packed_pool.tile([P, SLOTS * P], U8, name="scales", align_bytes=64)
-            codes_of[i], scales_of[i] = codes, scales
-            for first_bank, end_bank in ((0, 2), (2, BANKS)):
-                columns = slice(first_bank * SLOTS_PER_BANK * P, end_bank * SLOTS_PER_BANK * P)
-                nc.vector.quantize_mx(
-                    out=codes[:, columns].bitcast(FP8X4),
-                    scales=scales[:, columns],
-                    in_=grouped_of[i][:, first_bank * BANK_K : end_bank * BANK_K],
-                )
+        def open_pair(i):
+            grouped_of[i] = grouped_pool.tile([P, BANKS * BANK_K], BF16, name="grouped", align_bytes=64)
+            codes_of[i] = packed_pool.tile([P, SLOTS * P], U32, name="codes", align_bytes=64)
+            scales_of[i] = packed_pool.tile([P, SLOTS * P], U8, name="scales", align_bytes=64)
+
+        def transpose_bank(i, bank):
+            xt = transposed_pool.tile([P, SLOTS_PER_BANK, HALVES, P], F32, name="xt")
+            members = [(local, g) for g in range(PASSES) for local in range(PAIR) if slot_of(local, g) // SLOTS_PER_BANK == bank]
+            for local, g in members:
+                o = slot_of(local, g) % SLOTS_PER_BANK
+                words = k_slab(PAIR * i + local, g).bitcast(F32)
+                for u in range(HALVES):
+                    nc.tensor.transpose(xt[:, o, u, :], words[:, u * P : (u + 1) * P], identity[:])
+            nc.scalar.copy(
+                out=grouped_of[i][:, bank * BANK_K : (bank + 1) * BANK_K]
+                .bitcast(F32)
+                .rearrange("p (o r u) -> p o r u", o=SLOTS_PER_BANK, u=HALVES),
+                in_=xt[:].rearrange("p o u r -> p o r u"),
+            )
+
+        def quantise_banks(i, first_bank, end_bank):
+            columns = slice(first_bank * SLOTS_PER_BANK * P, end_bank * SLOTS_PER_BANK * P)
+            nc.vector.quantize_mx(
+                out=codes_of[i][:, columns].bitcast(FP8X4),
+                scales=scales_of[i][:, columns],
+                in_=grouped_of[i][:, first_bank * BANK_K : end_bank * BANK_K],
+            )
 
         def multiply_pair(i):
             gate = gate_pool.tile([P, PAIR, D], F32, name="gate")
@@ -113,7 +120,8 @@ def tile_updatefunction_pb_t_kernel(tc, node_state, message, h_tilda, mask, w_z,
             for local in range(PAIR):
                 acc = sum_pool.tile([P, D], F32, name="acc")
                 for g in range(PASSES):
-                    rows = slice((local * PASSES + g) * P, (local * PASSES + g + 1) * P)
+                    slot = slot_of(local, g)
+                    rows = slice(slot * P, (slot + 1) * P)
                     nc.tensor.matmul_mx(
                         out=acc[:],
                         lhsT=codes_of[i][:, rows].bitcast(FP8X4),
@@ -197,14 +205,25 @@ def tile_updatefunction_pb_t_kernel(tc, node_state, message, h_tilda, mask, w_z,
         nc.sync.dma_start(out=mask_bf16[:], in_=mask_rows)
         w_raw = consts.tile([P, PASSES, PACK, D], BF16)
         pass_rows = [w_z[g * K_PASS : (g + 1) * K_PASS, :] for g in range(M_PASSES)] + [u_z]
-        for g in range(PASSES):
+
+        def load_weights(g):
             nc.sync.dma_start(
                 out=w_raw[:, g].rearrange("p (u e) c -> p u (e c)", e=2),
                 in_=pass_rows[g].rearrange("(u p e) c -> p u (e c)", p=P, e=2),
             )
-        load_chunk(0, piece_tiles=PAIR)
+
+        open_chunk(0)
+        load_weights(0)
+        load_rows(m_chunks, m_rows, 0, PAIR)
+        load_weights(1)
+        load_rows(h_chunks, h_rows, 0, PAIR)
+        load_weights(2)
+        load_rows(m_chunks, m_rows, PAIR, PAIR)
+        load_rows(h_chunks, h_rows, PAIR, PAIR)
+        load_rows(ht_chunks, ht_rows, 0, PAIR)
+        load_rows(ht_chunks, ht_rows, PAIR, PAIR)
         for c in range(1, LOAD_AHEAD):
-            load_chunk(c, piece_tiles=CHUNK_TILES)
+            load_chunk(c)
 
         identity = consts.tile([P, P], F32)
         make_identity(nc, identity[:])
@@ -234,18 +253,28 @@ def tile_updatefunction_pb_t_kernel(tc, node_state, message, h_tilda, mask, w_z,
                 in_=w_grouped[:, g].rearrange("p c t -> p (c t)"),
             )
 
+        open_pair(0)
         regroup_weights(0)
-        for g in range(1, PASSES):
-            regroup_weights(g)
-            quantise_weights(g - 1)
-        quantise_weights(PASSES - 1)
+        transpose_bank(0, 0)
+        transpose_bank(0, 1)
+        quantise_weights(0)
+        regroup_weights(1)
+        quantise_banks(0, 0, 2)
+        quantise_weights(1)
+        transpose_bank(0, 2)
+        regroup_weights(2)
+        quantise_weights(2)
+        quantise_banks(0, 2, BANKS)
+        difference_on_vector(0)
 
-        for i in range(PAIRS + 2):
+        for i in range(1, PAIRS + 2):
             c_next = i // CHUNK_PAIRS + LOAD_AHEAD
-            if i % CHUNK_PAIRS == 0 and c_next < CHUNKS:
-                load_chunk(c_next, piece_tiles=CHUNK_TILES)
+            if i % CHUNK_PAIRS == 1 and c_next < CHUNKS:
+                load_chunk(c_next)
             if i < PAIRS:
-                transpose_pair(i)
+                open_pair(i)
+                for bank in range(BANKS):
+                    transpose_bank(i, bank)
             if 1 <= i <= PAIRS:
                 open_difference_on_tensor(i - 1)
                 multiply_pair(i - 1)
@@ -254,4 +283,5 @@ def tile_updatefunction_pb_t_kernel(tc, node_state, message, h_tilda, mask, w_z,
                 blend_pair(i - 2)
             if i < PAIRS:
                 difference_on_vector(i)
-                quantise_pair(i)
+                quantise_banks(i, 0, 2)
+                quantise_banks(i, 2, BANKS)

@@ -32,6 +32,8 @@ CHUNK_TILES = 4
 CHUNK_PAIRS = CHUNK_TILES // PAIR
 CHUNKS = TILES // CHUNK_TILES
 LOAD_AHEAD = 3
+GPSIMD_COLUMNS = slice(0, 192)
+VECTOR_COLUMNS = slice(192, D)
 W_VECTOR_COLUMNS = 336
 
 FLOPS = 2 * ROWS * (DM + D) * D
@@ -59,7 +61,7 @@ def tile_updatefunction_pb_t_kernel(tc, node_state, message, h_tilda, mask, w_z,
         tc.psum_pool(name="differences", bufs=3) as difference_pool,
     ):
         m_chunks, h_chunks, ht_chunks = {}, {}, {}
-        grouped_of, codes_of, scales_of, gate_of, blend_of, tensor_difference_of = {}, {}, {}, {}, {}, {}
+        grouped_of, codes_of, scales_of, gate_of, tensor_difference_of = {}, {}, {}, {}, {}
 
         def open_chunk(c):
             m_chunks[c] = inputs.tile([P, CHUNK_TILES, DM], BF16, name="m%d" % c)
@@ -162,21 +164,22 @@ def tile_updatefunction_pb_t_kernel(tc, node_state, message, h_tilda, mask, w_z,
                     stop=True,
                 )
 
-        def difference_on_vector(i):
-            blend = blend_pool.tile([P, PAIR, D], F32, name="blend")
-            blend_of[i] = blend
+        def differences_of(i):
+            return grouped_of[i][:, : 2 * D].bitcast(F32)
+
+        def difference_on(engine, i, columns):
             if tensor_tiles(i) < PAIR:
-                nc.vector.tensor_tensor(
-                    out=blend[:, 1, :],
-                    in0=pair_of(ht_chunks, i)[:, 1, :],
-                    in1=pair_of(h_chunks, i)[:, 1, :],
+                engine.tensor_tensor(
+                    out=differences_of(i)[:, columns],
+                    in0=pair_of(ht_chunks, i)[:, 1, columns],
+                    in1=pair_of(h_chunks, i)[:, 1, columns],
                     op=ALU.subtract,
                 )
 
         def blend_pair(i):
-            blend, gate, h_pair = blend_of[i], gate_of[i], pair_of(h_chunks, i)
+            blend, gate, h_pair = blend_pool.tile([P, PAIR, D], F32, name="blend"), gate_of[i], pair_of(h_chunks, i)
             differences = [
-                tensor_difference_of[i, local][:] if local < tensor_tiles(i) else blend[:, local, :]
+                tensor_difference_of[i, local][:] if local < tensor_tiles(i) else differences_of(i)
                 for local in range(PAIR)
             ]
             for local in range(PAIR):
@@ -265,7 +268,7 @@ def tile_updatefunction_pb_t_kernel(tc, node_state, message, h_tilda, mask, w_z,
         regroup_weights(2)
         quantise_weights(2)
         quantise_banks(0, 2, BANKS)
-        difference_on_vector(0)
+        difference_on(nc.gpsimd, 0, GPSIMD_COLUMNS)
 
         for i in range(1, PAIRS + 2):
             c_next = i // CHUNK_PAIRS + LOAD_AHEAD
@@ -281,7 +284,9 @@ def tile_updatefunction_pb_t_kernel(tc, node_state, message, h_tilda, mask, w_z,
                 close_difference_on_tensor(i - 1)
             if i >= 2:
                 blend_pair(i - 2)
+            if i <= PAIRS:
+                difference_on(nc.vector, i - 1, VECTOR_COLUMNS)
             if i < PAIRS:
-                difference_on_vector(i)
                 quantise_banks(i, 0, 2)
                 quantise_banks(i, 2, BANKS)
+                difference_on(nc.gpsimd, i, GPSIMD_COLUMNS)

@@ -32,9 +32,8 @@ CHUNK_TILES = 4
 CHUNK_PAIRS = CHUNK_TILES // PAIR
 CHUNKS = TILES // CHUNK_TILES
 LOAD_AHEAD = 3
-GPSIMD_COLUMNS = slice(0, 192)
-VECTOR_COLUMNS = slice(192, D)
-W_VECTOR_COLUMNS = 336
+GPSIMD_COLUMNS = 192
+W_VECTOR_COLUMNS = 368
 
 FLOPS = 2 * ROWS * (DM + D) * D
 
@@ -61,7 +60,7 @@ def tile_updatefunction_pb_t_kernel(tc, node_state, message, h_tilda, mask, w_z,
         tc.psum_pool(name="differences", bufs=3) as difference_pool,
     ):
         m_chunks, h_chunks, ht_chunks = {}, {}, {}
-        grouped_of, codes_of, scales_of, gate_of, tensor_difference_of = {}, {}, {}, {}, {}
+        grouped_of, codes_of, scales_of, sum_of, gate_of, tensor_difference_of = {}, {}, {}, {}, {}, {}
 
         def open_chunk(c):
             m_chunks[c] = inputs.tile([P, CHUNK_TILES, DM], BF16, name="m%d" % c)
@@ -74,10 +73,11 @@ def tile_updatefunction_pb_t_kernel(tc, node_state, message, h_tilda, mask, w_z,
                 out=chunks[c][:, first : first + count, :], in_=rows[:, first_tile : first_tile + count, :]
             )
 
-        def load_chunk(c):
+        def load_chunk(c, piece_tiles):
             open_chunk(c)
-            for chunks, rows in ((m_chunks, m_rows), (h_chunks, h_rows), (ht_chunks, ht_rows)):
-                load_rows(chunks, rows, c * CHUNK_TILES, CHUNK_TILES)
+            for first_tile in range(c * CHUNK_TILES, (c + 1) * CHUNK_TILES, piece_tiles):
+                for chunks, rows in ((m_chunks, m_rows), (h_chunks, h_rows), (ht_chunks, ht_rows)):
+                    load_rows(chunks, rows, first_tile, piece_tiles)
 
         def k_slab(t, g):
             c, local = divmod(t, CHUNK_TILES)
@@ -116,24 +116,27 @@ def tile_updatefunction_pb_t_kernel(tc, node_state, message, h_tilda, mask, w_z,
                 in_=grouped_of[i][:, first_bank * BANK_K : end_bank * BANK_K],
             )
 
-        def multiply_pair(i):
-            gate = gate_pool.tile([P, PAIR, D], F32, name="gate")
-            gate_of[i] = gate
+        def open_sums(i):
+            gate_of[i] = gate_pool.tile([P, PAIR, D], F32, name="gate")
             for local in range(PAIR):
-                acc = sum_pool.tile([P, D], F32, name="acc")
-                for g in range(PASSES):
-                    slot = slot_of(local, g)
-                    rows = slice(slot * P, (slot + 1) * P)
-                    nc.tensor.matmul_mx(
-                        out=acc[:],
-                        lhsT=codes_of[i][:, rows].bitcast(FP8X4),
-                        lhsT_scale=scales_of[i][:, rows],
-                        rhs=w_codes[:, g, :].bitcast(FP8X4),
-                        rhs_scale=w_scales[:, g, :],
-                        start=(g == 0),
-                        stop=(g == PASSES - 1),
-                    )
-                nc.scalar.activation(out=gate[:, local, :], in_=acc[:], func=ACT.Sigmoid)
+                sum_of[i, local] = sum_pool.tile([P, D], F32, name="acc")
+
+        def multiply(i, local, passes):
+            for g in passes:
+                slot = slot_of(local, g)
+                rows = slice(slot * P, (slot + 1) * P)
+                nc.tensor.matmul_mx(
+                    out=sum_of[i, local][:],
+                    lhsT=codes_of[i][:, rows].bitcast(FP8X4),
+                    lhsT_scale=scales_of[i][:, rows],
+                    rhs=w_codes[:, g, :].bitcast(FP8X4),
+                    rhs_scale=w_scales[:, g, :],
+                    start=(g == 0),
+                    stop=(g == PASSES - 1),
+                )
+
+        def make_gate(i, local):
+            nc.scalar.activation(out=gate_of[i][:, local, :], in_=sum_of[i, local][:], func=ACT.Sigmoid)
 
         def tensor_tiles(i):
             return PAIR if i % 5 == 0 and i > 0 else 1
@@ -164,11 +167,14 @@ def tile_updatefunction_pb_t_kernel(tc, node_state, message, h_tilda, mask, w_z,
                     stop=True,
                 )
 
+        def gpsimd_columns(i):
+            return GPSIMD_COLUMNS * tensor_tiles(i - 1)
+
         def differences_of(i):
             return grouped_of[i][:, : 2 * D].bitcast(F32)
 
         def difference_on(engine, i, columns):
-            if tensor_tiles(i) < PAIR:
+            if tensor_tiles(i) < PAIR and columns.start < columns.stop:
                 engine.tensor_tensor(
                     out=differences_of(i)[:, columns],
                     in0=pair_of(ht_chunks, i)[:, 1, columns],
@@ -205,7 +211,6 @@ def tile_updatefunction_pb_t_kernel(tc, node_state, message, h_tilda, mask, w_z,
                 nc.sync.dma_start(out=out_rows[:, t, :], in_=blend[:, local, :])
 
         mask_bf16 = consts.tile([P, TILES], BF16)
-        nc.sync.dma_start(out=mask_bf16[:], in_=mask_rows)
         w_raw = consts.tile([P, PASSES, PACK, D], BF16)
         pass_rows = [w_z[g * K_PASS : (g + 1) * K_PASS, :] for g in range(M_PASSES)] + [u_z]
 
@@ -224,22 +229,23 @@ def tile_updatefunction_pb_t_kernel(tc, node_state, message, h_tilda, mask, w_z,
         load_rows(m_chunks, m_rows, PAIR, PAIR)
         load_rows(h_chunks, h_rows, PAIR, PAIR)
         load_rows(ht_chunks, ht_rows, 0, PAIR)
+        nc.sync.dma_start(out=mask_bf16[:], in_=mask_rows)
         load_rows(ht_chunks, ht_rows, PAIR, PAIR)
-        for c in range(1, LOAD_AHEAD):
-            load_chunk(c)
+        load_chunk(1, PAIR)
+        for c in range(2, LOAD_AHEAD):
+            load_chunk(c, CHUNK_TILES)
 
+        warm = consts.tile([P, 1], F32)
+        nc.vector.memset(warm[:], 0.0)
+        nc.scalar.activation(out=warm[:], in_=warm[:], func=ACT.Sigmoid)
         identity = consts.tile([P, P], F32)
         make_identity(nc, identity[:])
         plus_identity = consts.tile([P, P], BF16)
         make_identity(nc, plus_identity[:])
         minus_identity = consts.tile([P, P], BF16)
         nc.vector.tensor_scalar_mul(out=minus_identity[:], in0=plus_identity[:], scalar1=-1.0)
-        warm = consts.tile([P, 1], F32)
-        nc.vector.memset(warm[:], 0.0)
-        nc.scalar.activation(out=warm[:], in_=warm[:], func=ACT.Sigmoid)
 
         mask_f32 = consts.tile([P, TILES], F32)
-        nc.vector.tensor_copy(out=mask_f32[:], in_=mask_bf16[:])
         w_grouped = consts.tile([P, PASSES, D, PACK], BF16, align_bytes=64)
         w_codes = consts.tile([P, PASSES, D], U32, align_bytes=64)
         w_scales = consts.tile([P, PASSES, D], U8, align_bytes=64)
@@ -265,28 +271,41 @@ def tile_updatefunction_pb_t_kernel(tc, node_state, message, h_tilda, mask, w_z,
         quantise_banks(0, 0, 2)
         quantise_weights(1)
         transpose_bank(0, 2)
+        open_sums(0)
+        for local in range(PAIR):
+            multiply(0, local, range(M_PASSES))
         regroup_weights(2)
-        quantise_weights(2)
         quantise_banks(0, 2, BANKS)
-        difference_on(nc.gpsimd, 0, GPSIMD_COLUMNS)
+        quantise_weights(2)
+        difference_on(nc.vector, 0, slice(0, D))
+        nc.vector.tensor_copy(out=mask_f32[:], in_=mask_bf16[:])
 
         for i in range(1, PAIRS + 2):
             c_next = i // CHUNK_PAIRS + LOAD_AHEAD
             if i % CHUNK_PAIRS == 1 and c_next < CHUNKS:
-                load_chunk(c_next)
+                load_chunk(c_next, CHUNK_TILES)
             if i < PAIRS:
                 open_pair(i)
                 for bank in range(BANKS):
                     transpose_bank(i, bank)
-            if 1 <= i <= PAIRS:
+            if i == 1:
+                for local in range(PAIR):
+                    multiply(0, local, range(M_PASSES, PASSES))
+                    make_gate(0, local)
+                open_difference_on_tensor(0)
+                close_difference_on_tensor(0)
+            elif i <= PAIRS:
+                open_sums(i - 1)
                 open_difference_on_tensor(i - 1)
-                multiply_pair(i - 1)
+                for local in range(PAIR):
+                    multiply(i - 1, local, range(PASSES))
+                    make_gate(i - 1, local)
                 close_difference_on_tensor(i - 1)
             if i >= 2:
                 blend_pair(i - 2)
-            if i <= PAIRS:
-                difference_on(nc.vector, i - 1, VECTOR_COLUMNS)
+            if 1 < i <= PAIRS:
+                difference_on(nc.vector, i - 1, slice(gpsimd_columns(i - 1), D))
             if i < PAIRS:
                 quantise_banks(i, 0, 2)
                 quantise_banks(i, 2, BANKS)
-                difference_on(nc.gpsimd, i, GPSIMD_COLUMNS)
+                difference_on(nc.gpsimd, i, slice(0, gpsimd_columns(i)))

@@ -32,7 +32,9 @@ CHUNK_TILES = 4
 CHUNK_PAIRS = CHUNK_TILES // PAIR
 CHUNKS = TILES // CHUNK_TILES
 LOAD_AHEAD = 3
-GPSIMD_COLUMNS = 192
+LAST_PIECES = 2
+GPSIMD_COLUMNS = (160, 416)
+W_RUN = 4
 W_VECTOR_COLUMNS = 368
 
 FLOPS = 2 * ROWS * (DM + D) * D
@@ -168,7 +170,7 @@ def tile_updatefunction_pb_t_kernel(tc, node_state, message, h_tilda, mask, w_z,
                 )
 
         def gpsimd_columns(i):
-            return GPSIMD_COLUMNS * tensor_tiles(i - 1)
+            return GPSIMD_COLUMNS[tensor_tiles(i - 1) - 1]
 
         def differences_of(i):
             return grouped_of[i][:, : 2 * D].bitcast(F32)
@@ -200,15 +202,18 @@ def tile_updatefunction_pb_t_kernel(tc, node_state, message, h_tilda, mask, w_z,
                 )
             for local in range(PAIR):
                 t = PAIR * i + local
-                nc.vector.scalar_tensor_tensor(
-                    out=blend[:, local, :],
-                    in0=h_pair[:, local, :],
-                    scalar=mask_f32[:, t : t + 1],
-                    in1=blend[:, local, :],
-                    op0=ALU.mult,
-                    op1=ALU.add,
-                )
-                nc.sync.dma_start(out=out_rows[:, t, :], in_=blend[:, local, :])
+                piece = D // LAST_PIECES if t == TILES - 1 else D
+                for first in range(0, D, piece):
+                    columns = slice(first, first + piece)
+                    nc.vector.scalar_tensor_tensor(
+                        out=blend[:, local, columns],
+                        in0=h_pair[:, local, columns],
+                        scalar=mask_f32[:, t : t + 1],
+                        in1=blend[:, local, columns],
+                        op0=ALU.mult,
+                        op1=ALU.add,
+                    )
+                    nc.sync.dma_start(out=out_rows[:, t, columns], in_=blend[:, local, columns])
 
         mask_bf16 = consts.tile([P, TILES], BF16)
         w_raw = consts.tile([P, PASSES, PACK, D], BF16)
@@ -251,9 +256,14 @@ def tile_updatefunction_pb_t_kernel(tc, node_state, message, h_tilda, mask, w_z,
         w_scales = consts.tile([P, PASSES, D], U8, align_bytes=64)
 
         def regroup_weights(g):
-            by_column = w_raw[:, g].rearrange("p t c -> p c t")
-            nc.vector.tensor_copy(out=w_grouped[:, g, :W_VECTOR_COLUMNS], in_=by_column[:, :W_VECTOR_COLUMNS])
-            nc.scalar.copy(out=w_grouped[:, g, W_VECTOR_COLUMNS:], in_=by_column[:, W_VECTOR_COLUMNS:])
+            for copy, columns in (
+                (nc.vector.tensor_copy, slice(0, W_VECTOR_COLUMNS)),
+                (nc.scalar.copy, slice(W_VECTOR_COLUMNS, D)),
+            ):
+                copy(
+                    out=w_grouped[:, g, columns].rearrange("p (c i) t -> p c t i", i=W_RUN),
+                    in_=w_raw[:, g, :, columns].rearrange("p t (c i) -> p c t i", i=W_RUN),
+                )
 
         def quantise_weights(g):
             nc.vector.quantize_mx(
@@ -272,8 +282,9 @@ def tile_updatefunction_pb_t_kernel(tc, node_state, message, h_tilda, mask, w_z,
         quantise_weights(1)
         transpose_bank(0, 2)
         open_sums(0)
-        for local in range(PAIR):
-            multiply(0, local, range(M_PASSES))
+        for g in range(M_PASSES):
+            for local in range(PAIR):
+                multiply(0, local, [g])
         regroup_weights(2)
         quantise_banks(0, 2, BANKS)
         quantise_weights(2)

@@ -33,8 +33,7 @@ CHUNK_PAIRS = CHUNK_TILES // PAIR
 CHUNKS = TILES // CHUNK_TILES
 LOAD_AHEAD = 3
 LAST_PIECES = 2
-GPSIMD_COLUMNS = (160, 416)
-W_RUN = 4
+GPSIMD_COLUMNS = 416
 W_VECTOR_COLUMNS = 368
 
 FLOPS = 2 * ROWS * (DM + D) * D
@@ -141,53 +140,48 @@ def tile_updatefunction_pb_t_kernel(tc, node_state, message, h_tilda, mask, w_z,
             nc.scalar.activation(out=gate_of[i][:, local, :], in_=sum_of[i, local][:], func=ACT.Sigmoid)
 
         def tensor_tiles(i):
-            return PAIR if i % 5 == 0 and i > 0 else 1
+            return PAIR if i % 2 == 1 else 1 if i % 8 == 6 else 0
 
         def pair_of(chunks, i):
             c, first = divmod(PAIR * i, CHUNK_TILES)
             return chunks[c][:, first : first + PAIR, :]
 
-        def open_difference_on_tensor(i):
-            for local in range(tensor_tiles(i)):
-                difference = difference_pool.tile([P, D], F32, name="difference")
-                tensor_difference_of[i, local] = difference
-                nc.tensor.matmul(
-                    out=difference[:],
-                    lhsT=plus_identity[:],
-                    rhs=pair_of(ht_chunks, i)[:, local, :],
-                    start=True,
-                    stop=False,
-                )
+        def open_difference_on_tensor(i, local):
+            difference = difference_pool.tile([P, D], F32, name="difference")
+            tensor_difference_of[i, local] = difference
+            nc.tensor.matmul(
+                out=difference[:], lhsT=plus_identity[:], rhs=pair_of(ht_chunks, i)[:, local, :], start=True, stop=False
+            )
 
-        def close_difference_on_tensor(i):
-            for local in range(tensor_tiles(i)):
-                nc.tensor.matmul(
-                    out=tensor_difference_of[i, local][:],
-                    lhsT=minus_identity[:],
-                    rhs=pair_of(h_chunks, i)[:, local, :],
-                    start=False,
-                    stop=True,
-                )
+        def close_difference_on_tensor(i, local):
+            nc.tensor.matmul(
+                out=tensor_difference_of[i, local][:],
+                lhsT=minus_identity[:],
+                rhs=pair_of(h_chunks, i)[:, local, :],
+                start=False,
+                stop=True,
+            )
 
         def gpsimd_columns(i):
-            return GPSIMD_COLUMNS[tensor_tiles(i - 1) - 1]
+            return GPSIMD_COLUMNS // max(1, PAIR - tensor_tiles(i))
 
         def differences_of(i):
-            return grouped_of[i][:, : 2 * D].bitcast(F32)
+            return grouped_of[i][:, : 2 * PAIR * D].bitcast(F32).rearrange("p (t d) -> p t d", t=PAIR)
 
         def difference_on(engine, i, columns):
-            if tensor_tiles(i) < PAIR and columns.start < columns.stop:
+            tiles = slice(tensor_tiles(i), PAIR)
+            if tensor_tiles(i) < PAIR:
                 engine.tensor_tensor(
-                    out=differences_of(i)[:, columns],
-                    in0=pair_of(ht_chunks, i)[:, 1, columns],
-                    in1=pair_of(h_chunks, i)[:, 1, columns],
+                    out=differences_of(i)[:, tiles, columns],
+                    in0=pair_of(ht_chunks, i)[:, tiles, columns],
+                    in1=pair_of(h_chunks, i)[:, tiles, columns],
                     op=ALU.subtract,
                 )
 
         def blend_pair(i):
             blend, gate, h_pair = blend_pool.tile([P, PAIR, D], F32, name="blend"), gate_of[i], pair_of(h_chunks, i)
             differences = [
-                tensor_difference_of[i, local][:] if local < tensor_tiles(i) else differences_of(i)
+                tensor_difference_of[i, local][:] if local < tensor_tiles(i) else differences_of(i)[:, local, :]
                 for local in range(PAIR)
             ]
             for local in range(PAIR):
@@ -256,14 +250,9 @@ def tile_updatefunction_pb_t_kernel(tc, node_state, message, h_tilda, mask, w_z,
         w_scales = consts.tile([P, PASSES, D], U8, align_bytes=64)
 
         def regroup_weights(g):
-            for copy, columns in (
-                (nc.vector.tensor_copy, slice(0, W_VECTOR_COLUMNS)),
-                (nc.scalar.copy, slice(W_VECTOR_COLUMNS, D)),
-            ):
-                copy(
-                    out=w_grouped[:, g, columns].rearrange("p (c i) t -> p c t i", i=W_RUN),
-                    in_=w_raw[:, g, :, columns].rearrange("p t (c i) -> p c t i", i=W_RUN),
-                )
+            by_column = w_raw[:, g].rearrange("p t c -> p c t")
+            nc.vector.tensor_copy(out=w_grouped[:, g, :W_VECTOR_COLUMNS], in_=by_column[:, :W_VECTOR_COLUMNS])
+            nc.scalar.copy(out=w_grouped[:, g, W_VECTOR_COLUMNS:], in_=by_column[:, W_VECTOR_COLUMNS:])
 
         def quantise_weights(g):
             nc.vector.quantize_mx(
@@ -299,19 +288,22 @@ def tile_updatefunction_pb_t_kernel(tc, node_state, message, h_tilda, mask, w_z,
                 open_pair(i)
                 for bank in range(BANKS):
                     transpose_bank(i, bank)
-            if i == 1:
+            around = (i, 0) if i % 2 == 1 else (i - 1, 1)
+            if i <= PAIRS:
+                if i > 1:
+                    open_sums(i - 1)
+                    if around[0] < PAIRS:
+                        open_difference_on_tensor(*around)
                 for local in range(PAIR):
-                    multiply(0, local, range(M_PASSES, PASSES))
-                    make_gate(0, local)
-                open_difference_on_tensor(0)
-                close_difference_on_tensor(0)
-            elif i <= PAIRS:
-                open_sums(i - 1)
-                open_difference_on_tensor(i - 1)
-                for local in range(PAIR):
-                    multiply(i - 1, local, range(PASSES))
+                    multiply(i - 1, local, range(PASSES) if i > 1 else range(M_PASSES, PASSES))
                     make_gate(i - 1, local)
-                close_difference_on_tensor(i - 1)
+                if i == 1:
+                    open_difference_on_tensor(*around)
+                if around[0] < PAIRS:
+                    close_difference_on_tensor(*around)
+                if tensor_tiles(i - 1) == 1:
+                    open_difference_on_tensor(i - 1, 0)
+                    close_difference_on_tensor(i - 1, 0)
             if i >= 2:
                 blend_pair(i - 2)
             if 1 < i <= PAIRS:

import concourse.mybir as mybir
from concourse.masks import make_identity

F32 = mybir.dt.float32
BF16 = mybir.dt.bfloat16
U32 = mybir.dt.uint32
U8 = mybir.dt.uint8
FP8X4 = mybir.dt.float8_e4m3fn_x4
ALU = mybir.AluOpType
ACT = mybir.ActivationFunctionType

P = 128
PACK = 4
K_PASS = P * PACK
HALVES = 2

ROWS = 4096
D = 512
DM = 1024
M_PASSES = DM // K_PASS
PASSES = M_PASSES + D // K_PASS

TILES = ROWS // P
PAIR = 2
PAIRS = TILES // PAIR
SLOTS = PAIR * PASSES
SLOTS_PER_BANK = 2
BANKS = SLOTS // SLOTS_PER_BANK
BANK_K = SLOTS_PER_BANK * P * PACK

CHUNK_TILES = 4
CHUNK_PAIRS = CHUNK_TILES // PAIR
CHUNKS = TILES // CHUNK_TILES
LOAD_AHEAD = 3
LAST_PIECES = 2
GPSIMD_COLUMNS = 416
W_VECTOR_COLUMNS = 368

FLOPS = 2 * ROWS * (DM + D) * D


def tile_updatefunction_pb_t_kernel(tc, node_state, message, h_tilda, mask, w_z, u_z, out):
    nc = tc.nc

    m_rows = message.rearrange("b (q t) k -> (b q) t k", t=TILES)
    h_rows = node_state.rearrange("b (q t) d -> (b q) t d", t=TILES)
    ht_rows = h_tilda.rearrange("(p t) d -> p t d", t=TILES)
    mask_rows = mask.rearrange("b (q t) -> (b q) t", t=TILES)
    out_rows = out.rearrange("b (q t) d -> (b q) t d", t=TILES)

    with (
        tc.manual_schedule(),
        tc.tile_pool(name="consts", bufs=1) as consts,
        tc.tile_pool(name="inputs", bufs=1) as inputs,
        tc.tile_pool(name="grouped", bufs=3) as grouped_pool,
        tc.tile_pool(name="packed", bufs=3) as packed_pool,
        tc.tile_pool(name="gates", bufs=3) as gate_pool,
        tc.tile_pool(name="blends", bufs=6) as blend_pool,
        tc.psum_pool(name="transposed", bufs=BANKS) as transposed_pool,
        tc.psum_pool(name="sums", bufs=PAIR) as sum_pool,
        tc.psum_pool(name="differences", bufs=3) as difference_pool,
    ):
        m_chunks, h_chunks, ht_chunks = {}, {}, {}
        grouped_of, codes_of, scales_of, sum_of, gate_of, tensor_difference_of = {}, {}, {}, {}, {}, {}

        def open_chunk(c):
            m_chunks[c] = inputs.tile([P, CHUNK_TILES, DM], BF16, name="m%d" % c)
            h_chunks[c] = inputs.tile([P, CHUNK_TILES, D], BF16, name="h%d" % c)
            ht_chunks[c] = inputs.tile([P, CHUNK_TILES, D], BF16, name="ht%d" % c)

        def load_rows(chunks, rows, first_tile, count):
            c, first = divmod(first_tile, CHUNK_TILES)
            nc.sync.dma_start(
                out=chunks[c][:, first : first + count, :], in_=rows[:, first_tile : first_tile + count, :]
            )

        def load_chunk(c, piece_tiles):
            open_chunk(c)
            for first_tile in range(c * CHUNK_TILES, (c + 1) * CHUNK_TILES, piece_tiles):
                for chunks, rows in ((m_chunks, m_rows), (h_chunks, h_rows), (ht_chunks, ht_rows)):
                    load_rows(chunks, rows, first_tile, piece_tiles)

        def k_slab(t, g):
            c, local = divmod(t, CHUNK_TILES)
            if g < M_PASSES:
                return m_chunks[c][:, local, g * K_PASS : (g + 1) * K_PASS]
            return h_chunks[c][:, local, :]

        def slot_of(local, g):
            return local * M_PASSES + g if g < M_PASSES else PAIR * M_PASSES + local

        def open_pair(i):
            grouped_of[i] = grouped_pool.tile([P, BANKS * BANK_K], BF16, name="grouped", align_bytes=64)
            codes_of[i] = packed_pool.tile([P, SLOTS * P], U32, name="codes", align_bytes=64)
            scales_of[i] = packed_pool.tile([P, SLOTS * P], U8, name="scales", align_bytes=64)

        def transpose_bank(i, bank):
            xt = transposed_pool.tile([P, SLOTS_PER_BANK, HALVES, P], F32, name="xt")
            members = [(local, g) for g in range(PASSES) for local in range(PAIR) if slot_of(local, g) // SLOTS_PER_BANK == bank]
            for local, g in members:
                o = slot_of(local, g) % SLOTS_PER_BANK
                words = k_slab(PAIR * i + local, g).bitcast(F32)
                for u in range(HALVES):
                    nc.tensor.transpose(xt[:, o, u, :], words[:, u * P : (u + 1) * P], identity[:])
            nc.scalar.copy(
                out=grouped_of[i][:, bank * BANK_K : (bank + 1) * BANK_K]
                .bitcast(F32)
                .rearrange("p (o r u) -> p o r u", o=SLOTS_PER_BANK, u=HALVES),
                in_=xt[:].rearrange("p o u r -> p o r u"),
            )

        def quantise_banks(i, first_bank, end_bank):
            columns = slice(first_bank * SLOTS_PER_BANK * P, end_bank * SLOTS_PER_BANK * P)
            nc.vector.quantize_mx(
                out=codes_of[i][:, columns].bitcast(FP8X4),
                scales=scales_of[i][:, columns],
                in_=grouped_of[i][:, first_bank * BANK_K : end_bank * BANK_K],
            )

        def open_sums(i):
            gate_of[i] = gate_pool.tile([P, PAIR, D], F32, name="gate")
            for local in range(PAIR):
                sum_of[i, local] = sum_pool.tile([P, D], F32, name="acc")

        def multiply(i, local, passes):
            for g in passes:
                slot = slot_of(local, g)
                rows = slice(slot * P, (slot + 1) * P)
                nc.tensor.matmul_mx(
                    out=sum_of[i, local][:],
                    lhsT=codes_of[i][:, rows].bitcast(FP8X4),
                    lhsT_scale=scales_of[i][:, rows],
                    rhs=w_codes[:, g, :].bitcast(FP8X4),
                    rhs_scale=w_scales[:, g, :],
                    start=(g == 0),
                    stop=(g == PASSES - 1),
                )

        def make_gate(i, local):
            nc.scalar.activation(out=gate_of[i][:, local, :], in_=sum_of[i, local][:], func=ACT.Sigmoid)

        def tensor_tiles(i):
            return PAIR if i % 2 == 1 else 1 if i % 8 == 6 else 0

        def pair_of(chunks, i):
            c, first = divmod(PAIR * i, CHUNK_TILES)
            return chunks[c][:, first : first + PAIR, :]

        def open_difference_on_tensor(i, local):
            difference = difference_pool.tile([P, D], F32, name="difference")
            tensor_difference_of[i, local] = difference
            nc.tensor.matmul(
                out=difference[:], lhsT=plus_identity[:], rhs=pair_of(ht_chunks, i)[:, local, :], start=True, stop=False
            )

        def close_difference_on_tensor(i, local):
            nc.tensor.matmul(
                out=tensor_difference_of[i, local][:],
                lhsT=minus_identity[:],
                rhs=pair_of(h_chunks, i)[:, local, :],
                start=False,
                stop=True,
            )

        def gpsimd_columns(i):
            return GPSIMD_COLUMNS // max(1, PAIR - tensor_tiles(i))

        def differences_of(i):
            return grouped_of[i][:, : 2 * PAIR * D].bitcast(F32).rearrange("p (t d) -> p t d", t=PAIR)

        def difference_on(engine, i, columns):
            tiles = slice(tensor_tiles(i), PAIR)
            if tensor_tiles(i) < PAIR:
                engine.tensor_tensor(
                    out=differences_of(i)[:, tiles, columns],
                    in0=pair_of(ht_chunks, i)[:, tiles, columns],
                    in1=pair_of(h_chunks, i)[:, tiles, columns],
                    op=ALU.subtract,
                )

        def blend_pair(i):
            blend, gate, h_pair = blend_pool.tile([P, PAIR, D], F32, name="blend"), gate_of[i], pair_of(h_chunks, i)
            differences = [
                tensor_difference_of[i, local][:] if local < tensor_tiles(i) else differences_of(i)[:, local, :]
                for local in range(PAIR)
            ]
            for local in range(PAIR):
                t = PAIR * i + local
                nc.vector.scalar_tensor_tensor(
                    out=blend[:, local, :],
                    in0=gate[:, local, :],
                    scalar=mask_f32[:, t : t + 1],
                    in1=differences[local],
                    op0=ALU.mult,
                    op1=ALU.mult,
                )
            for local in range(PAIR):
                t = PAIR * i + local
                piece = D // LAST_PIECES if t == TILES - 1 else D
                for first in range(0, D, piece):
                    columns = slice(first, first + piece)
                    nc.vector.scalar_tensor_tensor(
                        out=blend[:, local, columns],
                        in0=h_pair[:, local, columns],
                        scalar=mask_f32[:, t : t + 1],
                        in1=blend[:, local, columns],
                        op0=ALU.mult,
                        op1=ALU.add,
                    )
                    nc.sync.dma_start(out=out_rows[:, t, columns], in_=blend[:, local, columns])

        mask_bf16 = consts.tile([P, TILES], BF16)
        w_raw = consts.tile([P, PASSES, PACK, D], BF16)
        pass_rows = [w_z[g * K_PASS : (g + 1) * K_PASS, :] for g in range(M_PASSES)] + [u_z]

        def load_weights(g):
            nc.sync.dma_start(
                out=w_raw[:, g].rearrange("p (u e) c -> p u (e c)", e=2),
                in_=pass_rows[g].rearrange("(u p e) c -> p u (e c)", p=P, e=2),
            )

        open_chunk(0)
        load_weights(0)
        load_rows(m_chunks, m_rows, 0, PAIR)
        load_weights(1)
        load_rows(h_chunks, h_rows, 0, PAIR)
        load_weights(2)
        load_rows(m_chunks, m_rows, PAIR, PAIR)
        load_rows(h_chunks, h_rows, PAIR, PAIR)
        load_rows(ht_chunks, ht_rows, 0, PAIR)
        nc.sync.dma_start(out=mask_bf16[:], in_=mask_rows)
        load_rows(ht_chunks, ht_rows, PAIR, PAIR)
        load_chunk(1, PAIR)
        for c in range(2, LOAD_AHEAD):
            load_chunk(c, CHUNK_TILES)

        warm = consts.tile([P, 1], F32)
        nc.vector.memset(warm[:], 0.0)
        nc.scalar.activation(out=warm[:], in_=warm[:], func=ACT.Sigmoid)
        identity = consts.tile([P, P], F32)
        make_identity(nc, identity[:])
        plus_identity = consts.tile([P, P], BF16)
        make_identity(nc, plus_identity[:])
        minus_identity = consts.tile([P, P], BF16)
        nc.vector.tensor_scalar_mul(out=minus_identity[:], in0=plus_identity[:], scalar1=-1.0)

        mask_f32 = consts.tile([P, TILES], F32)
        w_grouped = consts.tile([P, PASSES, D, PACK], BF16, align_bytes=64)
        w_codes = consts.tile([P, PASSES, D], U32, align_bytes=64)
        w_scales = consts.tile([P, PASSES, D], U8, align_bytes=64)

        def regroup_weights(g):
            by_column = w_raw[:, g].rearrange("p t c -> p c t")
            nc.vector.tensor_copy(out=w_grouped[:, g, :W_VECTOR_COLUMNS], in_=by_column[:, :W_VECTOR_COLUMNS])
            nc.scalar.copy(out=w_grouped[:, g, W_VECTOR_COLUMNS:], in_=by_column[:, W_VECTOR_COLUMNS:])

        def quantise_weights(g):
            nc.vector.quantize_mx(
                out=w_codes[:, g, :].bitcast(FP8X4),
                scales=w_scales[:, g, :],
                in_=w_grouped[:, g].rearrange("p c t -> p (c t)"),
            )

        open_pair(0)
        regroup_weights(0)
        transpose_bank(0, 0)
        transpose_bank(0, 1)
        quantise_weights(0)
        regroup_weights(1)
        quantise_banks(0, 0, 2)
        quantise_weights(1)
        transpose_bank(0, 2)
        open_sums(0)
        for g in range(M_PASSES):
            for local in range(PAIR):
                multiply(0, local, [g])
        regroup_weights(2)
        quantise_banks(0, 2, BANKS)
        quantise_weights(2)
        difference_on(nc.vector, 0, slice(0, D))
        nc.vector.tensor_copy(out=mask_f32[:], in_=mask_bf16[:])

        for i in range(1, PAIRS + 2):
            c_next = i // CHUNK_PAIRS + LOAD_AHEAD
            if i % CHUNK_PAIRS == 1 and c_next < CHUNKS:
                load_chunk(c_next, CHUNK_TILES)
            if i < PAIRS:
                open_pair(i)
                for bank in range(BANKS):
                    transpose_bank(i, bank)
            around = (i, 0) if i % 2 == 1 else (i - 1, 1)
            if i <= PAIRS:
                if i > 1:
                    open_sums(i - 1)
                    if around[0] < PAIRS:
                        open_difference_on_tensor(*around)
                for local in range(PAIR):
                    multiply(i - 1, local, range(PASSES) if i > 1 else range(M_PASSES, PASSES))
                    make_gate(i - 1, local)
                if i == 1:
                    open_difference_on_tensor(*around)
                if around[0] < PAIRS:
                    close_difference_on_tensor(*around)
                if tensor_tiles(i - 1) == 1:
                    open_difference_on_tensor(i - 1, 0)
                    close_difference_on_tensor(i - 1, 0)
            if i >= 2:
                blend_pair(i - 2)
            if 1 < i <= PAIRS:
                difference_on(nc.vector, i - 1, slice(gpsimd_columns(i - 1), D))
            if i < PAIRS:
                quantise_banks(i, 0, 2)
                quantise_banks(i, 2, BANKS)
                difference_on(nc.gpsimd, i, slice(0, gpsimd_columns(i)))
